import numpy as np
import ml_dtypes

BF16 = ml_dtypes.bfloat16


def bf(x):
    return np.asarray(x, np.float32).astype(BF16)


def f32(x):
    return np.asarray(x, np.float32)


def f64(x):
    return np.asarray(x).astype(np.float64)


def striped(idx):
    return np.tile(idx.reshape(-1, 16).T, (8, 1))


C, S, K, N = 128, 512, 4, 2048
LN_EPS = 1e-5


def setup_inputs():
    return {
        "x": f32(np.random.standard_normal((C, S))),
        "ew": f32(np.random.uniform(0.2, 1.0, (1, N))),
        "conv_w": bf(np.random.standard_normal((C, C)) / np.sqrt(C)),
        "conv_b": f32(0.1 * np.random.standard_normal((C, 1))),
        "mlp_w": bf(np.random.standard_normal((C, C)) / np.sqrt(C)),
        "mlp_b": f32(0.1 * np.random.standard_normal((C, 1))),
        "ln_gain": f32(1.0 + 0.1 * np.random.standard_normal((C, 1))),
        "ln_bias": f32(0.1 * np.random.standard_normal((C, 1))),
        "offs": striped(np.concatenate([np.random.permutation(S) for _ in range(-(-(N) // S))])[:N]),
    }


def reference(x, ew, conv_w, conv_b, mlp_w, mlp_b, ln_gain, ln_bias, offs):
    idx = offs[:16].T.reshape(-1)
    e = f64(ew)
    deg = 1.0 + e.reshape(K, S).sum(axis=0, keepdims=True)
    dinv = 1.0 / np.sqrt(deg)
    y = f64(x) * dinv
    msg = y[:, idx] * e
    z = (y + msg.reshape(C, K, S).sum(axis=1)) * dinv
    u = f64(conv_w).T @ z + f64(conv_b)
    v = f64(mlp_w).T @ u + f64(mlp_b)
    mu = v.mean(axis=0, keepdims=True)
    d = v - mu
    var = (d * d).mean(axis=0, keepdims=True)
    return np.maximum(d / np.sqrt(var + LN_EPS) * f64(ln_gain) + f64(ln_bias), 0.0)

@@ -1,0 +1,95 @@
+import concourse.mybir as mybir
+
+F32 = mybir.dt.float32
+BF16 = mybir.dt.bfloat16
+U16 = mybir.dt.uint16
+ADD = mybir.AluOpType.add
+MULT = mybir.AluOpType.mult
+SUBTRACT = mybir.AluOpType.subtract
+ACT = mybir.ActivationFunctionType
+
+C = 128
+S = 512
+K = 4
+N = K * S
+LN_EPS = 1e-5
+
+FLOPS = 2 * 2 * C * C * S
+
+
+def tile_gcn_zencoder_kernel(
+    tc, x, ew, conv_w, conv_b, mlp_w, mlp_b, ln_gain, ln_bias, offs, out
+):
+    nc = tc.nc
+    with (
+        tc.tile_pool(name="held", bufs=1) as held,
+        tc.psum_pool(name="psum", bufs=1) as psum,
+    ):
+        ew_all = [held.tile([C, S], F32, name=f"ew_all{k}") for k in range(K)]
+        for k in range(K):
+            queue = nc.sync if k % 2 == 0 else nc.scalar
+            queue.dma_start(ew_all[k][:], ew[0, k * S : (k + 1) * S].partition_broadcast(C))
+        x_sb = held.tile([C, S], F32)
+        nc.scalar.dma_start(x_sb[:], x)
+        offsets = held.tile([C, N // 16], U16, name="offsets")
+        nc.sync.dma_start(offsets[:], offs)
+        conv_w_sb = held.tile([C, C], BF16)
+        nc.sync.dma_start(conv_w_sb[:], conv_w)
+        mlp_w_sb = held.tile([C, C], BF16)
+        nc.scalar.dma_start(mlp_w_sb[:], mlp_w)
+        conv_b_sb = held.tile([C, 1], F32)
+        nc.sync.dma_start(conv_b_sb[:], conv_b)
+        mlp_b_sb = held.tile([C, 1], F32)
+        nc.scalar.dma_start(mlp_b_sb[:], mlp_b)
+        ln_gain_sb = held.tile([C, 1], F32)
+        nc.sync.dma_start(ln_gain_sb[:], ln_gain)
+        ln_bias_sb = held.tile([C, 1], F32)
+        nc.scalar.dma_start(ln_bias_sb[:], ln_bias)
+
+        mean_w = held.tile([C, C], F32)
+        nc.gpsimd.memset(mean_w[:], 1.0 / C)
+
+        ew_sum = held.tile([C, S], F32)
+        nc.vector.tensor_tensor(ew_sum[:], ew_all[0][:], ew_all[1][:], ADD)
+        nc.vector.tensor_tensor(ew_sum[:], ew_sum[:], ew_all[2][:], ADD)
+        nc.vector.tensor_tensor(ew_sum[:], ew_sum[:], ew_all[3][:], ADD)
+        dinv = held.tile([C, S], F32)
+        nc.scalar.activation(dinv[:], ew_sum[:], ACT.Abs_reciprocal_sqrt, bias=1.0)
+        y = held.tile([C, S], F32)
+        nc.vector.tensor_tensor(y[:], x_sb[:], dinv[:], MULT)
+
+        total = held.tile([C, S], F32)
+        for k in range(K):
+            msg = held.tile([C, S], F32, name=f"msg{k}")
+            picked = y[:].indirect(offsets[:, k * (S // 16) : (k + 1) * (S // 16)])
+            nc.vector.tensor_tensor(msg[:], picked, ew_all[k][:], MULT)
+            nc.vector.tensor_tensor(total[:], (y if k == 0 else total)[:], msg[:], ADD)
+        z = held.tile([C, S], BF16)
+        nc.vector.tensor_tensor(z[:], total[:], dinv[:], MULT)
+
+        u_ps = psum.tile([C, S], F32)
+        nc.tensor.matmul(u_ps[:], conv_w_sb[:], z[:], start=True, stop=True)
+        u = held.tile([C, S], BF16)
+        nc.scalar.activation(u[:], u_ps[:], ACT.Identity, bias=conv_b_sb[:])
+        v_ps = psum.tile([C, S], F32)
+        nc.tensor.matmul(v_ps[:], mlp_w_sb[:], u[:], start=True, stop=True)
+        v = held.tile([C, S], F32)
+        nc.scalar.activation(v[:], v_ps[:], ACT.Identity, bias=mlp_b_sb[:])
+
+        mu_ps = psum.tile([C, S], F32)
+        nc.tensor.matmul(mu_ps[:], mean_w[:], v[:], start=True, stop=True)
+        d = held.tile([C, S], F32)
+        nc.vector.tensor_tensor(d[:], v[:], mu_ps[:], SUBTRACT)
+        d_sq = held.tile([C, S], F32)
+        nc.scalar.activation(d_sq[:], d[:], ACT.Square)
+        var_ps = psum.tile([C, S], F32)
+        nc.tensor.matmul(var_ps[:], mean_w[:], d_sq[:], start=True, stop=True)
+        rstd = held.tile([C, S], F32)
+        nc.scalar.activation(rstd[:], var_ps[:], ACT.Abs_reciprocal_sqrt, bias=LN_EPS)
+        normed = held.tile([C, S], F32)
+        nc.vector.tensor_tensor(normed[:], d[:], rstd[:], MULT)
+        result = held.tile([C, S], F32)
+        nc.scalar.activation(
+            result[:], normed[:], ACT.Relu, bias=ln_bias_sb[:], scale=ln_gain_sb[:]
+        )
+        nc.sync.dma_start(out, result[:])

@@ -7,6 +7,7 @@ ADD = mybir.AluOpType.add
 MULT = mybir.AluOpType.mult
 SUBTRACT = mybir.AluOpType.subtract
 ACT = mybir.ActivationFunctionType
+X_AXIS = mybir.AxisListType.X
 
 C = 128
 S = 512
@@ -25,36 +26,53 @@ def tile_gcn_zencoder_kernel(
         tc.tile_pool(name="held", bufs=1) as held,
         tc.psum_pool(name="psum", bufs=1) as psum,
     ):
+        ew_rows = held.tile([K, S], F32)
+        nc.sync.dma_start(ew_rows[:], ew.rearrange("o (k s) -> (o k) s", k=K))
+        x_sb = held.tile([C, S], F32)
+        nc.scalar.dma_start(x_sb[:], x)
+        mlp_w_sb = held.tile([C, C], BF16)
+        nc.sync.dma_start(mlp_w_sb[:], mlp_w)
+        offsets = held.tile([C, N // 16], U16, name="offsets")
+        nc.sync.dma_start(offsets[:], offs)
         ew_all = [held.tile([C, S], F32, name=f"ew_all{k}") for k in range(K)]
         for k in range(K):
             queue = nc.sync if k % 2 == 0 else nc.scalar
             queue.dma_start(ew_all[k][:], ew[0, k * S : (k + 1) * S].partition_broadcast(C))
-        x_sb = held.tile([C, S], F32)
-        nc.scalar.dma_start(x_sb[:], x)
-        offsets = held.tile([C, N // 16], U16, name="offsets")
-        nc.sync.dma_start(offsets[:], offs)
         conv_w_sb = held.tile([C, C], BF16)
         nc.sync.dma_start(conv_w_sb[:], conv_w)
-        mlp_w_sb = held.tile([C, C], BF16)
-        nc.scalar.dma_start(mlp_w_sb[:], mlp_w)
-        conv_b_sb = held.tile([C, 1], F32)
-        nc.sync.dma_start(conv_b_sb[:], conv_b)
         mlp_b_sb = held.tile([C, 1], F32)
-        nc.scalar.dma_start(mlp_b_sb[:], mlp_b)
+        nc.gpsimd.dma_start(mlp_b_sb[:], mlp_b)
+        conv_b_sb = held.tile([C, 1], F32)
+        nc.gpsimd.dma_start(conv_b_sb[:], conv_b)
         ln_gain_sb = held.tile([C, 1], F32)
-        nc.sync.dma_start(ln_gain_sb[:], ln_gain)
+        nc.gpsimd.dma_start(ln_gain_sb[:], ln_gain)
         ln_bias_sb = held.tile([C, 1], F32)
-        nc.scalar.dma_start(ln_bias_sb[:], ln_bias)
+        nc.gpsimd.dma_start(ln_bias_sb[:], ln_bias)
 
+        ones_rows = held.tile([K, C], F32)
+        nc.gpsimd.memset(ones_rows[:], 1.0)
         mean_w = held.tile([C, C], F32)
         nc.gpsimd.memset(mean_w[:], 1.0 / C)
 
-        ew_sum = held.tile([C, S], F32)
-        nc.vector.tensor_tensor(ew_sum[:], ew_all[0][:], ew_all[1][:], ADD)
-        nc.vector.tensor_tensor(ew_sum[:], ew_sum[:], ew_all[2][:], ADD)
-        nc.vector.tensor_tensor(ew_sum[:], ew_sum[:], ew_all[3][:], ADD)
+        w_sum = held.tile([C, 1], F32)
+        nc.vector.reduce_sum(w_sum[:], mlp_w_sb[:], axis=X_AXIS)
+        w_mean = held.tile([C, 1], F32)
+        nc.vector.tensor_scalar(w_mean[:], w_sum[:], 1.0 / C, None, MULT)
+        w_centred = held.tile([C, C], F32)
+        nc.vector.tensor_scalar(w_centred[:], mlp_w_sb[:], w_mean[:], None, SUBTRACT)
+        w_hi = held.tile([C, C], BF16)
+        nc.vector.tensor_copy(w_hi[:], w_centred[:])
+        w_lo = held.tile([C, C], BF16)
+        nc.vector.tensor_tensor(w_lo[:], w_centred[:], w_hi[:], SUBTRACT)
+        b_mean_ps = psum.tile([C, 1], F32)
+        nc.tensor.matmul(b_mean_ps[:], mean_w[:], mlp_b_sb[:], start=True, stop=True)
+        b_centred = held.tile([C, 1], F32)
+        nc.vector.tensor_tensor(b_centred[:], mlp_b_sb[:], b_mean_ps[:], SUBTRACT)
+
+        ew_sum_ps = psum.tile([C, S], F32)
+        nc.tensor.matmul(ew_sum_ps[:], ones_rows[:], ew_rows[:], start=True, stop=True)
         dinv = held.tile([C, S], F32)
-        nc.scalar.activation(dinv[:], ew_sum[:], ACT.Abs_reciprocal_sqrt, bias=1.0)
+        nc.scalar.activation(dinv[:], ew_sum_ps[:], ACT.Abs_reciprocal_sqrt, bias=1.0)
         y = held.tile([C, S], F32)
         nc.vector.tensor_tensor(y[:], x_sb[:], dinv[:], MULT)
 
@@ -71,25 +89,20 @@ def tile_gcn_zencoder_kernel(
         nc.tensor.matmul(u_ps[:], conv_w_sb[:], z[:], start=True, stop=True)
         u = held.tile([C, S], BF16)
         nc.scalar.activation(u[:], u_ps[:], ACT.Identity, bias=conv_b_sb[:])
-        v_ps = psum.tile([C, S], F32)
-        nc.tensor.matmul(v_ps[:], mlp_w_sb[:], u[:], start=True, stop=True)
-        v = held.tile([C, S], F32)
-        nc.scalar.activation(v[:], v_ps[:], ACT.Identity, bias=mlp_b_sb[:])
+        d_ps = psum.tile([C, S], F32)
+        nc.tensor.matmul(d_ps[:], w_hi[:], u[:], start=True, stop=False)
+        nc.tensor.matmul(d_ps[:], w_lo[:], u[:], start=False, stop=True)
 
-        mu_ps = psum.tile([C, S], F32)
-        nc.tensor.matmul(mu_ps[:], mean_w[:], v[:], start=True, stop=True)
-        d = held.tile([C, S], F32)
-        nc.vector.tensor_tensor(d[:], v[:], mu_ps[:], SUBTRACT)
         d_sq = held.tile([C, S], F32)
-        nc.scalar.activation(d_sq[:], d[:], ACT.Square)
+        nc.scalar.activation(d_sq[:], d_ps[:], ACT.Square, bias=b_centred[:])
         var_ps = psum.tile([C, S], F32)
         nc.tensor.matmul(var_ps[:], mean_w[:], d_sq[:], start=True, stop=True)
+        d_gain = held.tile([C, S], F32)
+        nc.vector.tensor_scalar(d_gain[:], d_ps[:], b_centred[:], ln_gain_sb[:], ADD, MULT)
         rstd = held.tile([C, S], F32)
         nc.scalar.activation(rstd[:], var_ps[:], ACT.Abs_reciprocal_sqrt, bias=LN_EPS)
         normed = held.tile([C, S], F32)
-        nc.vector.tensor_tensor(normed[:], d[:], rstd[:], MULT)
+        nc.vector.tensor_tensor(normed[:], d_gain[:], rstd[:], MULT)
         result = held.tile([C, S], F32)
-        nc.scalar.activation(
-            result[:], normed[:], ACT.Relu, bias=ln_bias_sb[:], scale=ln_gain_sb[:]
-        )
+        nc.scalar.activation(result[:], normed[:], ACT.Relu, bias=ln_bias_sb[:])
         nc.sync.dma_start(out, result[:])

@@ -1,10 +1,12 @@
 import concourse.mybir as mybir
+from concourse.masks import make_identity
 
 F32 = mybir.dt.float32
 BF16 = mybir.dt.bfloat16
 U16 = mybir.dt.uint16
 ADD = mybir.AluOpType.add
 MULT = mybir.AluOpType.mult
+MAX = mybir.AluOpType.max
 SUBTRACT = mybir.AluOpType.subtract
 ACT = mybir.ActivationFunctionType
 X_AXIS = mybir.AxisListType.X
@@ -13,6 +15,8 @@ C = 128
 S = 512
 K = 4
 N = K * S
+H = 2
+W = S // H
 LN_EPS = 1e-5
 
 FLOPS = 2 * 2 * C * C * S
@@ -24,7 +28,9 @@ def tile_gcn_zencoder_kernel(
     nc = tc.nc
     with (
         tc.tile_pool(name="held", bufs=1) as held,
-        tc.psum_pool(name="psum", bufs=1) as psum,
+        tc.tile_pool(name="block", bufs=H) as block,
+        tc.tile_pool(name="messages", bufs=1) as messages,
+        tc.psum_pool(name="psum_block", bufs=H) as psum_block,
     ):
         ew_rows = held.tile([K, S], F32)
         nc.sync.dma_start(ew_rows[:], ew.rearrange("o (k s) -> (o k) s", k=K))
@@ -38,21 +44,19 @@ def tile_gcn_zencoder_kernel(
         for k in range(K):
             queue = nc.sync if k % 2 == 0 else nc.scalar
             queue.dma_start(ew_all[k][:], ew[0, k * S : (k + 1) * S].partition_broadcast(C))
+        vectors = (mlp_b, ln_gain, conv_b, ln_bias)
+        vector_rows = held.tile([len(vectors), C], F32)
+        for j, vector in enumerate(vectors):
+            nc.sync.dma_start(vector_rows[j : j + 1, :], vector.rearrange("c o -> o c"))
         conv_w_sb = held.tile([C, C], BF16)
         nc.sync.dma_start(conv_w_sb[:], conv_w)
-        mlp_b_sb = held.tile([C, 1], F32)
-        nc.gpsimd.dma_start(mlp_b_sb[:], mlp_b)
-        conv_b_sb = held.tile([C, 1], F32)
-        nc.gpsimd.dma_start(conv_b_sb[:], conv_b)
-        ln_gain_sb = held.tile([C, 1], F32)
-        nc.gpsimd.dma_start(ln_gain_sb[:], ln_gain)
-        ln_bias_sb = held.tile([C, 1], F32)
-        nc.gpsimd.dma_start(ln_bias_sb[:], ln_bias)
 
         ones_rows = held.tile([K, C], F32)
         nc.gpsimd.memset(ones_rows[:], 1.0)
         mean_w = held.tile([C, C], F32)
         nc.gpsimd.memset(mean_w[:], 1.0 / C)
+        identity = held.tile([C, C], F32)
+        make_identity(nc, identity[:])
 
         w_sum = held.tile([C, 1], F32)
         nc.vector.reduce_sum(w_sum[:], mlp_w_sb[:], axis=X_AXIS)
@@ -64,45 +68,75 @@ def tile_gcn_zencoder_kernel(
         nc.vector.tensor_copy(w_hi[:], w_centred[:])
         w_lo = held.tile([C, C], BF16)
         nc.vector.tensor_tensor(w_lo[:], w_centred[:], w_hi[:], SUBTRACT)
-        b_mean_ps = psum.tile([C, 1], F32)
-        nc.tensor.matmul(b_mean_ps[:], mean_w[:], mlp_b_sb[:], start=True, stop=True)
-        b_centred = held.tile([C, 1], F32)
-        nc.vector.tensor_tensor(b_centred[:], mlp_b_sb[:], b_mean_ps[:], SUBTRACT)
 
-        ew_sum_ps = psum.tile([C, S], F32)
-        nc.tensor.matmul(ew_sum_ps[:], ones_rows[:], ew_rows[:], start=True, stop=True)
         dinv = held.tile([C, S], F32)
-        nc.scalar.activation(dinv[:], ew_sum_ps[:], ACT.Abs_reciprocal_sqrt, bias=1.0)
         y = held.tile([C, S], F32)
-        nc.vector.tensor_tensor(y[:], x_sb[:], dinv[:], MULT)
+        for h in range(H):
+            cols = slice(h * W, (h + 1) * W)
+            ew_sum_ps = psum_block.tile([C, W], F32, tag="column_stat")
+            nc.tensor.matmul(ew_sum_ps[:], ones_rows[:], ew_rows[:, cols], start=True, stop=True)
+            nc.scalar.activation(dinv[:, cols], ew_sum_ps[:], ACT.Abs_reciprocal_sqrt, bias=1.0)
+            nc.vector.tensor_tensor(y[:, cols], x_sb[:, cols], dinv[:, cols], MULT)
 
-        total = held.tile([C, S], F32)
-        for k in range(K):
-            msg = held.tile([C, S], F32, name=f"msg{k}")
-            picked = y[:].indirect(offsets[:, k * (S // 16) : (k + 1) * (S // 16)])
-            nc.vector.tensor_tensor(msg[:], picked, ew_all[k][:], MULT)
-            nc.vector.tensor_tensor(total[:], (y if k == 0 else total)[:], msg[:], ADD)
-        z = held.tile([C, S], BF16)
-        nc.vector.tensor_tensor(z[:], total[:], dinv[:], MULT)
+        vector_cols_ps = psum_block.tile([C, len(vectors)], F32, tag="column_stat")
+        nc.tensor.matmul(
+            vector_cols_ps[:],
+            vector_rows[:],
+            identity[: len(vectors), : len(vectors)],
+            start=True,
+            stop=True,
+        )
+        vector_cols = held.tile([C, len(vectors)], F32)
+        nc.vector.tensor_copy(vector_cols[:], vector_cols_ps[:])
+        mlp_b_sb, ln_gain_sb, conv_b_sb, ln_bias_sb = [
+            vector_cols[:, j : j + 1] for j in range(len(vectors))
+        ]
+        b_mean_ps = psum_block.tile([C, 1], F32, tag="column_stat")
+        nc.tensor.matmul(b_mean_ps[:], mean_w[:], mlp_b_sb, start=True, stop=True)
+        b_centred = held.tile([C, 1], F32)
+        nc.vector.tensor_tensor(b_centred[:], mlp_b_sb, b_mean_ps[:], SUBTRACT)
+        b_gain = held.tile([C, 1], F32)
+        nc.vector.tensor_tensor(b_gain[:], b_centred[:], ln_gain_sb, MULT)
 
-        u_ps = psum.tile([C, S], F32)
-        nc.tensor.matmul(u_ps[:], conv_w_sb[:], z[:], start=True, stop=True)
-        u = held.tile([C, S], BF16)
-        nc.scalar.activation(u[:], u_ps[:], ACT.Identity, bias=conv_b_sb[:])
-        d_ps = psum.tile([C, S], F32)
-        nc.tensor.matmul(d_ps[:], w_hi[:], u[:], start=True, stop=False)
-        nc.tensor.matmul(d_ps[:], w_lo[:], u[:], start=False, stop=True)
+        for h in range(H):
+            cols = slice(h * W, (h + 1) * W)
 
-        d_sq = held.tile([C, S], F32)
-        nc.scalar.activation(d_sq[:], d_ps[:], ACT.Square, bias=b_centred[:])
-        var_ps = psum.tile([C, S], F32)
-        nc.tensor.matmul(var_ps[:], mean_w[:], d_sq[:], start=True, stop=True)
-        d_gain = held.tile([C, S], F32)
-        nc.vector.tensor_scalar(d_gain[:], d_ps[:], b_centred[:], ln_gain_sb[:], ADD, MULT)
-        rstd = held.tile([C, S], F32)
-        nc.scalar.activation(rstd[:], var_ps[:], ACT.Abs_reciprocal_sqrt, bias=LN_EPS)
-        normed = held.tile([C, S], F32)
-        nc.vector.tensor_tensor(normed[:], d_gain[:], rstd[:], MULT)
-        result = held.tile([C, S], F32)
-        nc.scalar.activation(result[:], normed[:], ACT.Relu, bias=ln_bias_sb[:])
-        nc.sync.dma_start(out, result[:])
+            total_ps = psum_block.tile([C, W], F32)
+            nc.tensor.matmul(total_ps[:], identity[:], y[:, cols], start=True, stop=False)
+            for k in range(K):
+                first = (k * S + h * W) // 16
+                msg = messages.tile([C, W], F32, name=f"msg{k}")
+                picked = y[:].indirect(offsets[:, first : first + W // 16])
+                nc.vector.tensor_tensor(msg[:], picked, ew_all[k][:, cols], MULT)
+                if k < K - 1:
+                    nc.tensor.matmul(
+                        total_ps[:], identity[:], msg[:], start=False, stop=(k == K - 2)
+                    )
+            total = block.tile([C, W], F32)
+            nc.vector.tensor_tensor(total[:], msg[:], total_ps[:], ADD)
+            z = block.tile([C, W], BF16)
+            nc.vector.tensor_tensor(z[:], total[:], dinv[:, cols], MULT)
+
+            u_ps = psum_block.tile([C, W], F32)
+            nc.tensor.matmul(u_ps[:], conv_w_sb[:], z[:], start=True, stop=True)
+            u = block.tile([C, W], BF16)
+            nc.scalar.activation(u[:], u_ps[:], ACT.Identity, bias=conv_b_sb)
+            d_ps = psum_block.tile([C, W], F32)
+            nc.tensor.matmul(d_ps[:], w_hi[:], u[:], start=True, stop=False)
+            nc.tensor.matmul(d_ps[:], w_lo[:], u[:], start=False, stop=True)
+
+            d_sq = block.tile([C, W], F32)
+            nc.scalar.activation(d_sq[:], d_ps[:], ACT.Square, bias=b_centred[:])
+            var_ps = psum_block.tile([C, W], F32, tag="column_stat")
+            nc.tensor.matmul(var_ps[:], mean_w[:], d_sq[:], start=True, stop=True)
+            d_gain = block.tile([C, W], F32)
+            nc.scalar.activation(
+                d_gain[:], d_ps[:], ACT.Identity, bias=b_gain[:], scale=ln_gain_sb
+            )
+            rstd = block.tile([C, W], F32)
+            nc.scalar.activation(rstd[:], var_ps[:], ACT.Abs_reciprocal_sqrt, bias=LN_EPS)
+            normed = block.tile([C, W], F32)
+            nc.vector.tensor_tensor(normed[:], d_gain[:], rstd[:], MULT)
+            result = block.tile([C, W], F32)
+            nc.vector.tensor_scalar(result[:], normed[:], ln_bias_sb, 0.0, ADD, MAX)
+            nc.sync.dma_start(out[:, cols], result[:])

@@ -20,6 +20,8 @@ W = S // H
 LN_EPS = 1e-5
 
 FLOPS = 2 * 2 * C * C * S
+D = 128
+MSG_BUFS = K * H
 
 
 def tile_gcn_zencoder_kernel(
@@ -29,34 +31,53 @@ def tile_gcn_zencoder_kernel(
     with (
         tc.tile_pool(name="held", bufs=1) as held,
         tc.tile_pool(name="block", bufs=H) as block,
-        tc.tile_pool(name="messages", bufs=1) as messages,
-        tc.psum_pool(name="psum_block", bufs=H) as psum_block,
+        tc.tile_pool(name="messages", bufs=MSG_BUFS) as messages,
+        tc.psum_pool(name="psum", bufs=2) as psum,
     ):
+        conv_w_sb = held.tile([C, C], BF16)
+        nc.sync.dma_start(conv_w_sb[:], conv_w)
         ew_rows = held.tile([K, S], F32)
         nc.sync.dma_start(ew_rows[:], ew.rearrange("o (k s) -> (o k) s", k=K))
-        x_sb = held.tile([C, S], F32)
-        nc.scalar.dma_start(x_sb[:], x)
         mlp_w_sb = held.tile([C, C], BF16)
         nc.sync.dma_start(mlp_w_sb[:], mlp_w)
+        x_sb = held.tile([C, S], F32)
+        nc.sync.dma_start(x_sb[:], x)
         offsets = held.tile([C, N // 16], U16, name="offsets")
         nc.sync.dma_start(offsets[:], offs)
         ew_all = [held.tile([C, S], F32, name=f"ew_all{k}") for k in range(K)]
         for k in range(K):
-            queue = nc.sync if k % 2 == 0 else nc.scalar
-            queue.dma_start(ew_all[k][:], ew[0, k * S : (k + 1) * S].partition_broadcast(C))
-        vectors = (mlp_b, ln_gain, conv_b, ln_bias)
-        vector_rows = held.tile([len(vectors), C], F32)
-        for j, vector in enumerate(vectors):
-            nc.sync.dma_start(vector_rows[j : j + 1, :], vector.rearrange("c o -> o c"))
-        conv_w_sb = held.tile([C, C], BF16)
-        nc.sync.dma_start(conv_w_sb[:], conv_w)
+            nc.sync.dma_start(ew_all[k][:], ew[0, k * S : (k + 1) * S].partition_broadcast(C))
+        conv_b_sb = held.tile([C, 1], F32)
+        nc.scalar.dma_start(conv_b_sb[:], conv_b)
+        mlp_b_sb = held.tile([C, 1], F32)
+        nc.scalar.dma_start(mlp_b_sb[:], mlp_b)
+        ln_gain_sb = held.tile([C, 1], F32)
+        nc.scalar.dma_start(ln_gain_sb[:], ln_gain)
+        ln_bias_sb = held.tile([C, 1], F32)
+        nc.scalar.dma_start(ln_bias_sb[:], ln_bias)
 
         ones_rows = held.tile([K, C], F32)
         nc.gpsimd.memset(ones_rows[:], 1.0)
+        identity = held.tile([C, C], BF16)
+        make_identity(nc, identity[:])
+        centre = held.tile([C, C], F32)
+        nc.gpsimd.tensor_scalar(centre[:], identity[:], -1.0 / C, None, ADD)
         mean_w = held.tile([C, C], F32)
         nc.gpsimd.memset(mean_w[:], 1.0 / C)
-        identity = held.tile([C, C], F32)
-        make_identity(nc, identity[:])
+
+        conv_wT_ps = psum.tile([C, C], F32, tag="prepare")
+        nc.tensor.matmul(conv_wT_ps[:], conv_w_sb[:], identity[:], start=True, stop=True)
+        conv_wT = held.tile([C, C], F32)
+        nc.scalar.copy(conv_wT[:], conv_wT_ps[:])
+
+        dinv = held.tile([C, S], F32)
+        y = held.tile([C, S], F32)
+        for piece in range(S // D):
+            cols = slice(piece * D, (piece + 1) * D)
+            ew_sum_ps = psum.tile([C, D], F32)
+            nc.tensor.matmul(ew_sum_ps[:], ones_rows[:], ew_rows[:, cols], start=True, stop=True)
+            nc.scalar.activation(dinv[:, cols], ew_sum_ps[:], ACT.Abs_reciprocal_sqrt, bias=1.0)
+            nc.vector.tensor_tensor(y[:, cols], x_sb[:, cols], dinv[:, cols], MULT)
 
         w_sum = held.tile([C, 1], F32)
         nc.vector.reduce_sum(w_sum[:], mlp_w_sb[:], axis=X_AXIS)
@@ -64,79 +85,51 @@ def tile_gcn_zencoder_kernel(
         nc.vector.tensor_scalar(w_mean[:], w_sum[:], 1.0 / C, None, MULT)
         w_centred = held.tile([C, C], F32)
         nc.vector.tensor_scalar(w_centred[:], mlp_w_sb[:], w_mean[:], None, SUBTRACT)
-        w_hi = held.tile([C, C], BF16)
-        nc.vector.tensor_copy(w_hi[:], w_centred[:])
-        w_lo = held.tile([C, C], BF16)
-        nc.vector.tensor_tensor(w_lo[:], w_centred[:], w_hi[:], SUBTRACT)
+        both_w_ps = psum.tile([C, C], F32, tag="prepare")
+        nc.tensor.matmul(both_w_ps[:], conv_wT[:], w_centred[:], start=True, stop=True)
+        both_w = held.tile([C, C], F32)
+        nc.scalar.copy(both_w[:], both_w_ps[:])
 
-        dinv = held.tile([C, S], F32)
-        y = held.tile([C, S], F32)
-        for h in range(H):
-            cols = slice(h * W, (h + 1) * W)
-            ew_sum_ps = psum_block.tile([C, W], F32, tag="column_stat")
-            nc.tensor.matmul(ew_sum_ps[:], ones_rows[:], ew_rows[:, cols], start=True, stop=True)
-            nc.scalar.activation(dinv[:, cols], ew_sum_ps[:], ACT.Abs_reciprocal_sqrt, bias=1.0)
-            nc.vector.tensor_tensor(y[:, cols], x_sb[:, cols], dinv[:, cols], MULT)
-
-        vector_cols_ps = psum_block.tile([C, len(vectors)], F32, tag="column_stat")
-        nc.tensor.matmul(
-            vector_cols_ps[:],
-            vector_rows[:],
-            identity[: len(vectors), : len(vectors)],
-            start=True,
-            stop=True,
-        )
-        vector_cols = held.tile([C, len(vectors)], F32)
-        nc.vector.tensor_copy(vector_cols[:], vector_cols_ps[:])
-        mlp_b_sb, ln_gain_sb, conv_b_sb, ln_bias_sb = [
-            vector_cols[:, j : j + 1] for j in range(len(vectors))
-        ]
-        b_mean_ps = psum_block.tile([C, 1], F32, tag="column_stat")
-        nc.tensor.matmul(b_mean_ps[:], mean_w[:], mlp_b_sb, start=True, stop=True)
-        b_centred = held.tile([C, 1], F32)
-        nc.vector.tensor_tensor(b_centred[:], mlp_b_sb, b_mean_ps[:], SUBTRACT)
+        both_b_ps = psum.tile([C, 1], F32, tag="prepare")
+        nc.tensor.matmul(both_b_ps[:], w_centred[:], conv_b_sb[:], start=True, stop=False)
+        nc.tensor.matmul(both_b_ps[:], centre[:], mlp_b_sb[:], start=False, stop=True)
+        both_b = held.tile([C, 1], F32)
+        nc.scalar.copy(both_b[:], both_b_ps[:])
         b_gain = held.tile([C, 1], F32)
-        nc.vector.tensor_tensor(b_gain[:], b_centred[:], ln_gain_sb, MULT)
+        nc.scalar.activation(b_gain[:], both_b_ps[:], ACT.Copy, scale=ln_gain_sb[:])
 
-        for h in range(H):
-            cols = slice(h * W, (h + 1) * W)
-
-            total_ps = psum_block.tile([C, W], F32)
-            nc.tensor.matmul(total_ps[:], identity[:], y[:, cols], start=True, stop=False)
-            for k in range(K):
+        blocks = [slice(h * W, (h + 1) * W) for h in range(H)]
+        summed_ps = [psum.tile([C, W], F32, name="summed_ps") for h in range(H)]
+        for k in range(K):
+            for h in range(H):
                 first = (k * S + h * W) // 16
-                msg = messages.tile([C, W], F32, name=f"msg{k}")
+                msg = messages.tile([C, W], F32)
                 picked = y[:].indirect(offsets[:, first : first + W // 16])
-                nc.vector.tensor_tensor(msg[:], picked, ew_all[k][:, cols], MULT)
-                if k < K - 1:
-                    nc.tensor.matmul(
-                        total_ps[:], identity[:], msg[:], start=False, stop=(k == K - 2)
-                    )
-            total = block.tile([C, W], F32)
-            nc.vector.tensor_tensor(total[:], msg[:], total_ps[:], ADD)
-            z = block.tile([C, W], BF16)
-            nc.vector.tensor_tensor(z[:], total[:], dinv[:, cols], MULT)
+                nc.vector.tensor_tensor(msg[:], picked, ew_all[k][:, blocks[h]], MULT)
+                if k == 0:
+                    with_self = messages.tile([C, W], F32)
+                    nc.vector.tensor_tensor(with_self[:], msg[:], y[:, blocks[h]], ADD)
+                    msg = with_self
+                nc.tensor.matmul(
+                    summed_ps[h][:], both_w[:], msg[:], start=(k == 0), stop=(k == K - 1)
+                )
 
-            u_ps = psum_block.tile([C, W], F32)
-            nc.tensor.matmul(u_ps[:], conv_w_sb[:], z[:], start=True, stop=True)
-            u = block.tile([C, W], BF16)
-            nc.scalar.activation(u[:], u_ps[:], ACT.Identity, bias=conv_b_sb)
-            d_ps = psum_block.tile([C, W], F32)
-            nc.tensor.matmul(d_ps[:], w_hi[:], u[:], start=True, stop=False)
-            nc.tensor.matmul(d_ps[:], w_lo[:], u[:], start=False, stop=True)
-
-            d_sq = block.tile([C, W], F32)
-            nc.scalar.activation(d_sq[:], d_ps[:], ACT.Square, bias=b_centred[:])
-            var_ps = psum_block.tile([C, W], F32, tag="column_stat")
-            nc.tensor.matmul(var_ps[:], mean_w[:], d_sq[:], start=True, stop=True)
-            d_gain = block.tile([C, W], F32)
-            nc.scalar.activation(
-                d_gain[:], d_ps[:], ACT.Identity, bias=b_gain[:], scale=ln_gain_sb
-            )
-            rstd = block.tile([C, W], F32)
-            nc.scalar.activation(rstd[:], var_ps[:], ACT.Abs_reciprocal_sqrt, bias=LN_EPS)
+        d, d_sq, var_ps, d_gain, rstd = [], [], [], [], []
+        for h in range(H):
+            d.append(block.tile([C, W], F32, name="d"))
+            nc.vector.tensor_tensor(d[h][:], summed_ps[h][:], dinv[:, blocks[h]], MULT)
+            d_sq.append(block.tile([C, W], F32, name="d_sq"))
+            nc.scalar.activation(d_sq[h][:], d[h][:], ACT.Square, bias=both_b[:])
+            var_ps.append(psum.tile([C, W], F32, name="var_ps"))
+            nc.tensor.matmul(var_ps[h][:], mean_w[:], d_sq[h][:], start=True, stop=True)
+        for h in range(H):
+            d_gain.append(block.tile([C, W], F32, name="d_gain"))
+            nc.vector.tensor_scalar(d_gain[h][:], d[h][:], ln_gain_sb[:], b_gain[:], MULT, ADD)
+        for h in range(H):
+            rstd.append(block.tile([C, W], F32, name="rstd"))
+            nc.scalar.activation(rstd[h][:], var_ps[h][:], ACT.Abs_reciprocal_sqrt, bias=LN_EPS)
             normed = block.tile([C, W], F32)
-            nc.vector.tensor_tensor(normed[:], d_gain[:], rstd[:], MULT)
+            nc.vector.tensor_tensor(normed[:], d_gain[h][:], rstd[h][:], MULT)
             result = block.tile([C, W], F32)
-            nc.vector.tensor_scalar(result[:], normed[:], ln_bias_sb, 0.0, ADD, MAX)
-            nc.sync.dma_start(out[:, cols], result[:])
+            nc.vector.tensor_scalar(result[:], normed[:], ln_bias_sb[:], 0.0, ADD, MAX)
+            nc.sync.dma_start(out[:, blocks[h]], result[:])

@@ -36,8 +36,9 @@ def tile_gcn_zencoder_kernel(
     ):
         conv_w_sb = held.tile([C, C], BF16)
         nc.sync.dma_start(conv_w_sb[:], conv_w)
-        ew_rows = held.tile([K, S], F32)
-        nc.sync.dma_start(ew_rows[:], ew.rearrange("o (k s) -> (o k) s", k=K))
+        ew_rows = held.tile([C, S], F32)
+        nc.gpsimd.memset(ew_rows[:], 0.0)
+        nc.sync.dma_start(ew_rows[:K, :], ew.rearrange("o (k s) -> (o k) s", k=K))
         mlp_w_sb = held.tile([C, C], BF16)
         nc.sync.dma_start(mlp_w_sb[:], mlp_w)
         x_sb = held.tile([C, S], F32)
@@ -56,14 +57,12 @@ def tile_gcn_zencoder_kernel(
         ln_bias_sb = held.tile([C, 1], F32)
         nc.scalar.dma_start(ln_bias_sb[:], ln_bias)
 
-        ones_rows = held.tile([K, C], F32)
-        nc.gpsimd.memset(ones_rows[:], 1.0)
+        mean_w = held.tile([C, C], F32)
+        nc.gpsimd.memset(mean_w[:], 1.0 / C)
         identity = held.tile([C, C], BF16)
         make_identity(nc, identity[:])
         centre = held.tile([C, C], F32)
         nc.gpsimd.tensor_scalar(centre[:], identity[:], -1.0 / C, None, ADD)
-        mean_w = held.tile([C, C], F32)
-        nc.gpsimd.memset(mean_w[:], 1.0 / C)
 
         conv_wT_ps = psum.tile([C, C], F32, tag="prepare")
         nc.tensor.matmul(conv_wT_ps[:], conv_w_sb[:], identity[:], start=True, stop=True)
@@ -74,9 +73,11 @@ def tile_gcn_zencoder_kernel(
         y = held.tile([C, S], F32)
         for piece in range(S // D):
             cols = slice(piece * D, (piece + 1) * D)
-            ew_sum_ps = psum.tile([C, D], F32)
-            nc.tensor.matmul(ew_sum_ps[:], ones_rows[:], ew_rows[:, cols], start=True, stop=True)
-            nc.scalar.activation(dinv[:, cols], ew_sum_ps[:], ACT.Abs_reciprocal_sqrt, bias=1.0)
+            ew_mean_ps = psum.tile([C, D], F32)
+            nc.tensor.matmul(ew_mean_ps[:], mean_w[:], ew_rows[:, cols], start=True, stop=True)
+            nc.scalar.activation(
+                dinv[:, cols], ew_mean_ps[:], ACT.Abs_reciprocal_sqrt, bias=1.0, scale=float(C)
+            )
             nc.vector.tensor_tensor(y[:, cols], x_sb[:, cols], dinv[:, cols], MULT)
 
         w_sum = held.tile([C, 1], F32)

@@ -69,17 +69,6 @@ def tile_gcn_zencoder_kernel(
         conv_wT = held.tile([C, C], F32)
         nc.scalar.copy(conv_wT[:], conv_wT_ps[:])
 
-        dinv = held.tile([C, S], F32)
-        y = held.tile([C, S], F32)
-        for piece in range(S // D):
-            cols = slice(piece * D, (piece + 1) * D)
-            ew_mean_ps = psum.tile([C, D], F32)
-            nc.tensor.matmul(ew_mean_ps[:], mean_w[:], ew_rows[:, cols], start=True, stop=True)
-            nc.scalar.activation(
-                dinv[:, cols], ew_mean_ps[:], ACT.Abs_reciprocal_sqrt, bias=1.0, scale=float(C)
-            )
-            nc.vector.tensor_tensor(y[:, cols], x_sb[:, cols], dinv[:, cols], MULT)
-
         w_sum = held.tile([C, 1], F32)
         nc.vector.reduce_sum(w_sum[:], mlp_w_sb[:], axis=X_AXIS)
         w_mean = held.tile([C, 1], F32)
@@ -99,20 +88,29 @@ def tile_gcn_zencoder_kernel(
         b_gain = held.tile([C, 1], F32)
         nc.scalar.activation(b_gain[:], both_b_ps[:], ACT.Copy, scale=ln_gain_sb[:])
 
+        dinv = held.tile([C, S], F32)
+        y = held.tile([C, S], F32)
+        for piece in range(S // D):
+            cols = slice(piece * D, (piece + 1) * D)
+            ew_mean_ps = psum.tile([C, D], F32)
+            nc.tensor.matmul(ew_mean_ps[:], mean_w[:], ew_rows[:, cols], start=True, stop=True)
+            nc.scalar.activation(
+                dinv[:, cols], ew_mean_ps[:], ACT.Abs_reciprocal_sqrt, bias=1.0, scale=float(C)
+            )
+            nc.vector.tensor_tensor(y[:, cols], x_sb[:, cols], dinv[:, cols], MULT)
+
         blocks = [slice(h * W, (h + 1) * W) for h in range(H)]
         summed_ps = [psum.tile([C, W], F32, name="summed_ps") for h in range(H)]
+        for h in range(H):
+            nc.tensor.matmul(summed_ps[h][:], both_w[:], y[:, blocks[h]], start=True, stop=False)
         for k in range(K):
             for h in range(H):
                 first = (k * S + h * W) // 16
                 msg = messages.tile([C, W], F32)
                 picked = y[:].indirect(offsets[:, first : first + W // 16])
                 nc.vector.tensor_tensor(msg[:], picked, ew_all[k][:, blocks[h]], MULT)
-                if k == 0:
-                    with_self = messages.tile([C, W], F32)
-                    nc.vector.tensor_tensor(with_self[:], msg[:], y[:, blocks[h]], ADD)
-                    msg = with_self
                 nc.tensor.matmul(
-                    summed_ps[h][:], both_w[:], msg[:], start=(k == 0), stop=(k == K - 1)
+                    summed_ps[h][:], both_w[:], msg[:], start=False, stop=(k == K - 1)
                 )
 
         d, d_sq, var_ps, d_gain, rstd = [], [], [], [], []

import concourse.mybir as mybir
from concourse.masks import make_identity

F32 = mybir.dt.float32
BF16 = mybir.dt.bfloat16
U16 = mybir.dt.uint16
ADD = mybir.AluOpType.add
MULT = mybir.AluOpType.mult
MAX = mybir.AluOpType.max
SUBTRACT = mybir.AluOpType.subtract
ACT = mybir.ActivationFunctionType
X_AXIS = mybir.AxisListType.X

C = 128
S = 512
K = 4
N = K * S
H = 2
W = S // H
LN_EPS = 1e-5

FLOPS = 2 * 2 * C * C * S
D = 128
MSG_BUFS = K * H


def tile_gcn_zencoder_kernel(
    tc, x, ew, conv_w, conv_b, mlp_w, mlp_b, ln_gain, ln_bias, offs, out
):
    nc = tc.nc
    with (
        tc.tile_pool(name="held", bufs=1) as held,
        tc.tile_pool(name="block", bufs=H) as block,
        tc.tile_pool(name="messages", bufs=MSG_BUFS) as messages,
        tc.psum_pool(name="psum", bufs=2) as psum,
    ):
        conv_w_sb = held.tile([C, C], BF16)
        nc.sync.dma_start(conv_w_sb[:], conv_w)
        ew_rows = held.tile([C, S], F32)
        nc.gpsimd.memset(ew_rows[:], 0.0)
        nc.sync.dma_start(ew_rows[:K, :], ew.rearrange("o (k s) -> (o k) s", k=K))
        mlp_w_sb = held.tile([C, C], BF16)
        nc.sync.dma_start(mlp_w_sb[:], mlp_w)
        x_sb = held.tile([C, S], F32)
        nc.sync.dma_start(x_sb[:], x)
        offsets = held.tile([C, N // 16], U16, name="offsets")
        nc.sync.dma_start(offsets[:], offs)
        ew_all = [held.tile([C, S], F32, name=f"ew_all{k}") for k in range(K)]
        for k in range(K):
            nc.sync.dma_start(ew_all[k][:], ew[0, k * S : (k + 1) * S].partition_broadcast(C))
        conv_b_sb = held.tile([C, 1], F32)
        nc.scalar.dma_start(conv_b_sb[:], conv_b)
        mlp_b_sb = held.tile([C, 1], F32)
        nc.scalar.dma_start(mlp_b_sb[:], mlp_b)
        ln_gain_sb = held.tile([C, 1], F32)
        nc.scalar.dma_start(ln_gain_sb[:], ln_gain)
        ln_bias_sb = held.tile([C, 1], F32)
        nc.scalar.dma_start(ln_bias_sb[:], ln_bias)

        mean_w = held.tile([C, C], F32)
        nc.gpsimd.memset(mean_w[:], 1.0 / C)
        identity = held.tile([C, C], BF16)
        make_identity(nc, identity[:])
        centre = held.tile([C, C], F32)
        nc.gpsimd.tensor_scalar(centre[:], identity[:], -1.0 / C, None, ADD)

        conv_wT_ps = psum.tile([C, C], F32, tag="prepare")
        nc.tensor.matmul(conv_wT_ps[:], conv_w_sb[:], identity[:], start=True, stop=True)
        conv_wT = held.tile([C, C], F32)
        nc.scalar.copy(conv_wT[:], conv_wT_ps[:])

        w_sum = held.tile([C, 1], F32)
        nc.vector.reduce_sum(w_sum[:], mlp_w_sb[:], axis=X_AXIS)
        w_mean = held.tile([C, 1], F32)
        nc.vector.tensor_scalar(w_mean[:], w_sum[:], 1.0 / C, None, MULT)
        w_centred = held.tile([C, C], F32)
        nc.vector.tensor_scalar(w_centred[:], mlp_w_sb[:], w_mean[:], None, SUBTRACT)
        both_w_ps = psum.tile([C, C], F32, tag="prepare")
        nc.tensor.matmul(both_w_ps[:], conv_wT[:], w_centred[:], start=True, stop=True)
        both_w = held.tile([C, C], F32)
        nc.scalar.copy(both_w[:], both_w_ps[:])

        both_b_ps = psum.tile([C, 1], F32, tag="prepare")
        nc.tensor.matmul(both_b_ps[:], w_centred[:], conv_b_sb[:], start=True, stop=False)
        nc.tensor.matmul(both_b_ps[:], centre[:], mlp_b_sb[:], start=False, stop=True)
        both_b = held.tile([C, 1], F32)
        nc.scalar.copy(both_b[:], both_b_ps[:])
        b_gain = held.tile([C, 1], F32)
        nc.scalar.activation(b_gain[:], both_b_ps[:], ACT.Copy, scale=ln_gain_sb[:])

        dinv = held.tile([C, S], F32)
        y = held.tile([C, S], F32)
        for piece in range(S // D):
            cols = slice(piece * D, (piece + 1) * D)
            ew_mean_ps = psum.tile([C, D], F32)
            nc.tensor.matmul(ew_mean_ps[:], mean_w[:], ew_rows[:, cols], start=True, stop=True)
            nc.scalar.activation(
                dinv[:, cols], ew_mean_ps[:], ACT.Abs_reciprocal_sqrt, bias=1.0, scale=float(C)
            )
            nc.vector.tensor_tensor(y[:, cols], x_sb[:, cols], dinv[:, cols], MULT)

        blocks = [slice(h * W, (h + 1) * W) for h in range(H)]
        summed_ps = [psum.tile([C, W], F32, name="summed_ps") for h in range(H)]
        for h in range(H):
            nc.tensor.matmul(summed_ps[h][:], both_w[:], y[:, blocks[h]], start=True, stop=False)
        for k in range(K):
            for h in range(H):
                first = (k * S + h * W) // 16
                msg = messages.tile([C, W], F32)
                picked = y[:].indirect(offsets[:, first : first + W // 16])
                nc.vector.tensor_tensor(msg[:], picked, ew_all[k][:, blocks[h]], MULT)
                nc.tensor.matmul(
                    summed_ps[h][:], both_w[:], msg[:], start=False, stop=(k == K - 1)
                )

        d, d_sq, var_ps, d_gain, rstd = [], [], [], [], []
        for h in range(H):
            d.append(block.tile([C, W], F32, name="d"))
            nc.vector.tensor_tensor(d[h][:], summed_ps[h][:], dinv[:, blocks[h]], MULT)
            d_sq.append(block.tile([C, W], F32, name="d_sq"))
            nc.scalar.activation(d_sq[h][:], d[h][:], ACT.Square, bias=both_b[:])
            var_ps.append(psum.tile([C, W], F32, name="var_ps"))
            nc.tensor.matmul(var_ps[h][:], mean_w[:], d_sq[h][:], start=True, stop=True)
        for h in range(H):
            d_gain.append(block.tile([C, W], F32, name="d_gain"))
            nc.vector.tensor_scalar(d_gain[h][:], d[h][:], ln_gain_sb[:], b_gain[:], MULT, ADD)
        for h in range(H):
            rstd.append(block.tile([C, W], F32, name="rstd"))
            nc.scalar.activation(rstd[h][:], var_ps[h][:], ACT.Abs_reciprocal_sqrt, bias=LN_EPS)
            normed = block.tile([C, W], F32)
            nc.vector.tensor_tensor(normed[:], d_gain[h][:], rstd[h][:], MULT)
            result = block.tile([C, W], F32)
            nc.vector.tensor_scalar(result[:], normed[:], ln_bias_sb[:], 0.0, ADD, MAX)
            nc.sync.dma_start(out[:, blocks[h]], result[:])
